import numpy as np
import ml_dtypes


def mxq(x, axis, fmt="e4m3"):
    dtype, down = {"e4m3": (ml_dtypes.float8_e4m3fn, 7), "e5m2": (ml_dtypes.float8_e5m2, 14)}[fmt]
    v = np.moveaxis(np.asarray(x, np.float32).astype(ml_dtypes.bfloat16).astype(np.float64), axis, -1)
    blocks = v.reshape(v.shape[:-1] + (-1, 32))
    amax = np.abs(blocks).max(-1, keepdims=True)
    byte = np.maximum(np.where(amax > 0, np.frexp(amax)[1] - 1 + 127, 0) - down, 1)
    scale = np.exp2(byte - 127.0)
    codes = (blocks / scale).astype(np.float32).astype(dtype).astype(np.float64)
    return np.moveaxis((codes * scale).reshape(v.shape), -1, axis)


WIDE = False


def mx_kscale(k):
    if not WIDE:
        return np.ones(k)
    levels = np.array([10, -10, 5, -5, 0])
    if k % 512:
        return np.exp2(np.random.permutation(np.resize(levels, k // 32))).repeat(32)
    a = np.empty((k // 512, 16))
    for p in range(k // 512):
        a[p, :8] = np.random.permutation(np.resize(levels, 8))
        for g in range(8):
            far = levels[np.abs(levels - a[p, g]) >= 10]
            a[p, g + 8] = far[np.random.randint(len(far))]
    return np.exp2(a.ravel()).repeat(32)


BF16 = ml_dtypes.bfloat16


def bf(x):
    return np.asarray(x, np.float32).astype(BF16)


def f64(x):
    return np.asarray(x).astype(np.float64)


B, T, D, E, F = 4, 768, 2048, 2048, 8192
EPS = 1e-6


def rms_norm(x, w):
    rms = np.sqrt(np.mean(x * x, axis=-1, keepdims=True) + EPS)
    return x / rms * w


def erf(v):
    a = np.minimum(np.abs(v), 6.0)
    z = 2.0 * a * a
    term = a.copy()
    tot = a.copy()
    for n in range(1, 110):
        term = term * z / (2 * n + 1)
        tot = tot + term
    return np.sign(v) * tot * np.exp(-a * a) * 2.0 / np.sqrt(np.pi)


def gelu_erf(v):
    return 0.5 * v * (1.0 + erf(v / np.sqrt(2.0)))


def setup_inputs():
    s, t = mx_kscale(E), mx_kscale(D)
    return {"attn": bf(np.random.standard_normal((B, T, E)) * 0.6 * s),
            "x": bf(np.random.standard_normal((B, T, D))),
            "wo": bf(np.random.standard_normal((E, D)) / np.sqrt(E) / s[:, None]),
            "bo": bf(np.random.standard_normal(D) * 0.1),
            "mlp_norm_w": bf((1.0 + 0.1 * np.random.standard_normal(D)) * t),
            "w1": bf(np.random.standard_normal((D, F)) / np.sqrt(D) / t[:, None]),
            "b1": bf(np.random.standard_normal(F) * 0.1)}


def reference(attn, x, wo, bo, mlp_norm_w, w1, b1):
    x_mid = f64(x) + (mxq(f64(attn), 2, "e4m3") @ mxq(f64(wo), 0, "e4m3")) + f64(bo)
    h = rms_norm(x_mid, f64(mlp_norm_w))
    g = gelu_erf((mxq(h, 2, "e4m3") @ mxq(f64(w1), 0, "e4m3")) + f64(b1))
    return x_mid, g

@@ -1,0 +1,324 @@
+import math
+from contextlib import ExitStack
+
+import concourse.mybir as mybir
+from concourse.masks import make_identity
+
+F32 = mybir.dt.float32
+BF16 = mybir.dt.bfloat16
+U32 = mybir.dt.uint32
+U8 = mybir.dt.uint8
+FP8X4 = mybir.dt.float8_e4m3fn_x4
+ALU = mybir.AluOpType
+ACT = mybir.ActivationFunctionType
+
+P = 128
+TOKENS = 3072
+D = 2048
+F = 8192
+EPS = 1e-6
+NT = TOKENS // P
+NG = D // 512
+NW = 512
+ND = D // NW
+NF = F // NW
+
+FLOPS = 2 * TOKENS * D * (D + F)
+
+MANUAL = False
+XB_ON_GPSIMD = False
+RAW_BUFS = 5
+
+
+def tile_tinyblock_pb_l_kernel(tc, attn, x, wo, bo, mlp_norm_w, w1, b1, out_0, out_1):
+    nc = tc.nc
+    attn_f = attn.flatten_outer_dims()
+    x_f = x.flatten_outer_dims()
+    xmid_f = out_0.flatten_outer_dims()
+    g_f = out_1.flatten_outer_dims()
+
+    with ExitStack() as ctx:
+        const = ctx.enter_context(tc.tile_pool(name="const", bufs=1))
+        keep = ctx.enter_context(tc.tile_pool(name="keep", bufs=1))
+        wst = ctx.enter_context(tc.tile_pool(name="wst", bufs=2))
+        work = ctx.enter_context(tc.tile_pool(name="work", bufs=2))
+        small = ctx.enter_context(tc.tile_pool(name="small", bufs=4))
+        psum = ctx.enter_context(tc.psum_pool(name="psum", bufs=4))
+        if MANUAL:
+            ctx.enter_context(tc.manual_schedule())
+
+        identf = const.tile([P, P], F32, name="identf")
+        make_identity(nc, identf[:])
+        neghalf = const.tile([P, 1], F32, name="neghalf")
+        nc.gpsimd.memset(neghalf[:], -0.5)
+        warm = const.tile([P, 1], F32, name="warm")
+        nc.gpsimd.memset(warm[:], 0.0)
+        warm2 = const.tile([P, 1], F32, name="warm2")
+        nc.scalar.activation(out=warm2[:], in_=warm[:], func=ACT.Gelu)
+        junk = const.tile([P, D // 2], BF16, name="junk")
+        bo_b = const.tile([P, D], BF16, name="bo_b")
+        gain_b = const.tile([P, D], BF16, name="gain_b")
+        b1_b = const.tile([P, F], BF16, name="b1_b")
+
+        woq = []
+        wos = []
+        for n in range(ND):
+            woq_t = keep.tile([P, NG, NW], U32, name="woq%d" % n, align_bytes=64)
+            wos_t = keep.tile([P, NW], U8, name="wos%d" % n, align_bytes=64)
+            woq.append(woq_t)
+            wos.append(wos_t)
+        hq = []
+        hs = []
+        for m in range(NT):
+            hq_t = keep.tile([P, NG, P], U32, name="hq%d" % m, align_bytes=64)
+            hs_t = keep.tile([P, P], U8, name="hs%d" % m, align_bytes=64)
+            hq.append(hq_t)
+            hs.append(hs_t)
+
+        units = [(0, n, g) for n in range(ND) for g in range(NG)] + [(1, n, g) for n in range(NF) for g in range(NG)]
+        raws = {}
+        grps = {}
+        w1q = {}
+        w1s = {}
+
+        def load_unit(k):
+            if k >= len(units):
+                return
+            kind, n, g = units[k]
+            src = w1 if kind else wo
+            raw = wst.tile([P, 4, NW], BF16, tag="wraw", bufs=RAW_BUFS)
+            nc.sync.dma_start(
+                out=raw[:],
+                in_=src[512 * g : 512 * (g + 1), NW * n : NW * (n + 1)].rearrange("(p j) c -> p j c", j=4),
+            )
+            raws[k] = raw
+
+        def group_unit(k, on_vector):
+            grp = wst.tile([P, NW, 4], BF16, tag="wgrp", bufs=3, align_bytes=64)
+            src = raws[k][:].rearrange("p j c -> p c j")
+            if on_vector:
+                nc.vector.tensor_copy(out=grp[:], in_=src)
+            else:
+                nc.scalar.copy(out=grp[:], in_=src)
+            grps[k] = grp
+
+        def quant_unit(k):
+            kind, n, g = units[k]
+            if kind:
+                if g == 0:
+                    wq_t = wst.tile([P, NG, NW], U32, tag="wq", bufs=2, align_bytes=64)
+                    ws_t = wst.tile([P, NW], U8, tag="wsc", bufs=2, align_bytes=64)
+                    w1q[n] = wq_t
+                    w1s[n] = ws_t
+                q, s = w1q[n], w1s[n]
+            else:
+                q, s = woq[n], wos[n]
+            nc.vector.quantize_mx(
+                out=q[:, g, :].bitcast(FP8X4),
+                scales=s[4 * g : P, :],
+                in_=grps[k][:].rearrange("p c j -> p (c j)"),
+            )
+
+        araw = {}
+        xraw = {}
+        agrp = {}
+        hgrp = {}
+        aq = {}
+        asc = {}
+        xm = {}
+        hb = {}
+        rstd = {}
+
+        def load_tok(i):
+            if i >= NT:
+                return
+            ar = work.tile([P, D], BF16, tag="araw", bufs=2)
+            nc.sync.dma_start(out=ar[:], in_=attn_f[P * i : P * (i + 1), :])
+            xr = work.tile([P, D], BF16, tag="xraw", bufs=2)
+            nc.sync.dma_start(out=xr[:], in_=x_f[P * i : P * (i + 1), :])
+            araw[i] = ar
+            xraw[i] = xr
+
+        def transpose_rows(src):
+            words = src[:].bitcast(F32)
+            grp = work.tile([P, NG, P, 4], BF16, tag="grp", bufs=3, align_bytes=64)
+            grp_w = grp[:].rearrange("p g r t -> p (g r t)").bitcast(F32).rearrange("p (g r u) -> p g r u", g=NG, u=2)
+            for b in range(2):
+                tp = psum.tile([P, 2, 2, P], F32, tag="tp")
+                for gg in range(2):
+                    g = 2 * b + gg
+                    for u in range(2):
+                        nc.tensor.transpose(tp[:, gg, u, :], words[:, 256 * g + u : 256 * (g + 1) : 2], identf[:])
+                nc.scalar.copy(out=grp_w[:, 2 * b : 2 * b + 2], in_=tp[:].rearrange("p g u r -> p g r u"))
+            return grp
+
+        def tr_a(i):
+            if 0 <= i < NT:
+                agrp[i] = transpose_rows(araw[i])
+
+        def tr_h(i):
+            if 0 <= i < NT:
+                hgrp[i] = transpose_rows(hb[i])
+
+        def make_xb(i):
+            if not 0 <= i < NT:
+                return
+            xm_t = work.tile([P, D], F32, tag="xm", bufs=3)
+            eng = nc.gpsimd if XB_ON_GPSIMD else nc.vector
+            eng.tensor_tensor(out=xm_t[:], in0=xraw[i][:], in1=bo_b[:], op=ALU.add)
+            xm[i] = xm_t
+
+        def quant_a(i):
+            if not 0 <= i < NT:
+                return
+            aq_t = work.tile([P, NG * P], U32, tag="aq", bufs=2, align_bytes=64)
+            as_t = work.tile([P, NG * P], U8, tag="asc", bufs=2, align_bytes=64)
+            nc.vector.quantize_mx(
+                out=aq_t[:].bitcast(FP8X4), scales=as_t[:], in_=agrp[i][:].rearrange("p g r t -> p (g r t)")
+            )
+            aq[i] = aq_t
+            asc[i] = as_t
+
+        def make_h(i):
+            if not 0 <= i < NT:
+                return
+            hb_t = work.tile([P, D], BF16, tag="hb", bufs=2)
+            nc.vector.scalar_tensor_tensor(
+                out=hb_t[:], in0=xm[i][:], scalar=rstd[i][:, 0:1], in1=gain_b[:], op0=ALU.mult, op1=ALU.mult
+            )
+            hb[i] = hb_t
+
+        def quant_h(i):
+            if not 0 <= i < NT:
+                return
+            for g in range(NG):
+                nc.vector.quantize_mx(
+                    out=hq[i][:, g, :].bitcast(FP8X4),
+                    scales=hs[i][4 * g : P, :],
+                    in_=hgrp[i][:, g].rearrange("p r t -> p (r t)"),
+                )
+
+        def stage1(i, mid):
+            sums = []
+            for n in range(ND):
+                cols = slice(NW * n, NW * (n + 1))
+                acc = psum.tile([P, NW], F32, tag="acc")
+                for g in range(NG):
+                    nc.tensor.matmul_mx(
+                        out=acc[:],
+                        lhsT=aq[i][:, P * g : P * (g + 1)].bitcast(FP8X4),
+                        lhsT_scale=asc[i][:, P * g : P * (g + 1)],
+                        rhs=woq[n][:, g, :].bitcast(FP8X4),
+                        rhs_scale=wos[n][4 * g : P, :],
+                        start=(g == 0),
+                        stop=(g == NG - 1),
+                    )
+                mid(n)
+                nc.vector.tensor_tensor(out=xm[i][:, cols], in0=acc[:], in1=xm[i][:, cols], op=ALU.add)
+                if n % 2 == 1:
+                    ss = small.tile([P, 1], F32, tag="ss%d" % (n // 2))
+                    nc.scalar.activation(
+                        out=junk[:],
+                        in_=xm[i][:, NW * (n - 1) : NW * (n + 1)],
+                        func=ACT.Square,
+                        scale=1.0 / math.sqrt(D),
+                        accum_out=ss[:],
+                    )
+                    sums.append(ss)
+            var = small.tile([P, 1], F32, tag="var")
+            nc.gpsimd.tensor_scalar(
+                out=var[:], in0=sums[0][:], scalar1=sums[1][:, 0:1], scalar2=EPS, op0=ALU.add, op1=ALU.add
+            )
+            rs = small.tile([P, 1], F32, tag="rstd")
+            nc.gpsimd.tensor_tensor(out=rs[:], in0=var[:], in1=neghalf[:], op=ALU.pow)
+            rstd[i] = rs
+            nc.sync.dma_start(out=xmid_f[P * i : P * (i + 1), :], in_=xm[i][:])
+
+        def nothing(n):
+            return
+
+        def prep_wo(n):
+            for g in range(NG):
+                k = NG * n + g
+                group_unit(k, g % 2 == 0)
+                load_unit(k + RAW_BUFS)
+                if g > 0:
+                    quant_unit(k - 1)
+            quant_unit(NG * n + NG - 1)
+
+        def prep_next_wo(n):
+            if n + 1 < ND:
+                prep_wo(n + 1)
+
+        load_tok(0)
+        for k in range(RAW_BUFS):
+            load_unit(k)
+        nc.sync.dma_start(out=bo_b[:], in_=bo.partition_broadcast(P))
+        load_tok(1)
+        nc.sync.dma_start(out=gain_b[:], in_=mlp_norm_w.partition_broadcast(P))
+        tr_a(0)
+        prep_wo(0)
+        quant_a(0)
+        make_xb(0)
+
+        NWO = ND * NG
+        for i in range(NT):
+            load_tok(i + 2)
+            tr_a(i + 1)
+            tr_h(i - 2)
+            make_xb(i + 1)
+            quant_a(i + 1)
+            make_h(i - 1)
+            quant_h(i - 2)
+            stage1(i, prep_next_wo if i == 0 else nothing)
+            if i >= 3 and i % 2 == 1 and (i - 3) // 2 < 2 * NG:
+                k = NWO + (i - 3) // 2
+                group_unit(k, False)
+                load_unit(k + RAW_BUFS)
+            if i >= 4 and i % 2 == 0 and (i - 4) // 2 < 2 * NG:
+                quant_unit(NWO + (i - 4) // 2)
+            if i == 8:
+                nc.sync.dma_start(out=b1_b[:], in_=b1.partition_broadcast(P))
+
+        ot = None
+        for n in range(NF):
+            cols = slice(NW * n, NW * (n + 1))
+            for m in range(NT):
+                idx = n * NT + m
+                if idx == 0:
+                    tr_h(NT - 2)
+                    make_h(NT - 1)
+                    quant_h(NT - 2)
+                if idx == 6:
+                    tr_h(NT - 1)
+                    quant_h(NT - 1)
+                if 1 <= n < NF - 1:
+                    k = NWO + NG * (n + 1) + m // 6
+                    if m % 6 == 0:
+                        group_unit(k, (m // 6) % 2 == 0)
+                        load_unit(k + RAW_BUFS)
+                    if m % 6 == 3:
+                        quant_unit(k)
+                acc = psum.tile([P, NW], F32, tag=("acc" if idx % 2 == 0 else "tp"))
+                for g in range(NG):
+                    nc.tensor.matmul_mx(
+                        out=acc[:],
+                        lhsT=hq[m][:, g, :].bitcast(FP8X4),
+                        lhsT_scale=hs[m][4 * g : P, :],
+                        rhs=w1q[n][:, g, :].bitcast(FP8X4),
+                        rhs_scale=w1s[n][4 * g : P, :],
+                        start=(g == 0),
+                        stop=(g == NG - 1),
+                    )
+                q = m % 4
+                if q == 0:
+                    ot = work.tile([P, 4, NW], F32, tag="xm", bufs=3)
+                nc.vector.tensor_tensor(out=ot[:, q, :], in0=acc[:], in1=b1_b[:, cols], op=ALU.add)
+                nc.scalar.activation(out=ot[:, q, :], in_=ot[:, q, :], func=ACT.Gelu)
+                last = n == NF - 1 and m >= NT - 4
+                if last:
+                    nc.sync.dma_start(out=g_f[P * m : P * (m + 1), cols], in_=ot[:, q, :])
+                elif q == 3:
+                    nc.sync.dma_start(
+                        out=g_f[P * (m - 3) : P * (m + 1), cols].rearrange("(q p) c -> p q c", p=P), in_=ot[:]
+                    )

@@ -28,6 +28,7 @@ FLOPS = 2 * TOKENS * D * (D + F)
 MANUAL = False
 XB_ON_GPSIMD = False
 RAW_BUFS = 5
+EARLY = 2
 
 
 def tile_tinyblock_pb_l_kernel(tc, attn, x, wo, bo, mlp_norm_w, w1, b1, out_0, out_1):
@@ -58,7 +59,6 @@ def tile_tinyblock_pb_l_kernel(tc, attn, x, wo, bo, mlp_norm_w, w1, b1, out_0, o
         junk = const.tile([P, D // 2], BF16, name="junk")
         bo_b = const.tile([P, D], BF16, name="bo_b")
         gain_b = const.tile([P, D], BF16, name="gain_b")
-        b1_b = const.tile([P, F], BF16, name="b1_b")
 
         woq = []
         wos = []
@@ -80,6 +80,8 @@ def tile_tinyblock_pb_l_kernel(tc, attn, x, wo, bo, mlp_norm_w, w1, b1, out_0, o
         grps = {}
         w1q = {}
         w1s = {}
+        b1c = {}
+        ready = set()
 
         def load_unit(k):
             if k >= len(units):
@@ -106,10 +108,13 @@ def tile_tinyblock_pb_l_kernel(tc, attn, x, wo, bo, mlp_norm_w, w1, b1, out_0, o
             kind, n, g = units[k]
             if kind:
                 if g == 0:
-                    wq_t = wst.tile([P, NG, NW], U32, tag="wq", bufs=2, align_bytes=64)
-                    ws_t = wst.tile([P, NW], U8, tag="wsc", bufs=2, align_bytes=64)
+                    wq_t = wst.tile([P, NG, NW], U32, tag="wq", bufs=3, align_bytes=64)
+                    ws_t = wst.tile([P, NW], U8, tag="wsc", bufs=3, align_bytes=64)
+                    b1_t = wst.tile([P, NW], BF16, tag="b1c", bufs=3)
+                    nc.sync.dma_start(out=b1_t[:], in_=b1[NW * n : NW * (n + 1)].partition_broadcast(P))
                     w1q[n] = wq_t
                     w1s[n] = ws_t
+                    b1c[n] = b1_t
                 q, s = w1q[n], w1s[n]
             else:
                 q, s = woq[n], wos[n]
@@ -118,6 +123,8 @@ def tile_tinyblock_pb_l_kernel(tc, attn, x, wo, bo, mlp_norm_w, w1, b1, out_0, o
                 scales=s[4 * g : P, :],
                 in_=grps[k][:].rearrange("p c j -> p (c j)"),
             )
+            if kind and g == NG - 1:
+                ready.add(n)
 
         araw = {}
         xraw = {}
@@ -261,6 +268,37 @@ def tile_tinyblock_pb_l_kernel(tc, attn, x, wo, bo, mlp_norm_w, w1, b1, out_0, o
         quant_a(0)
         make_xb(0)
 
+        count = [0]
+
+        def block(n, m):
+            idx = count[0]
+            count[0] = idx + 1
+            cols = slice(NW * n, NW * (n + 1))
+            acc = psum.tile([P, NW], F32, tag=("acc" if idx % 2 == 0 else "tp"))
+            for g in range(NG):
+                nc.tensor.matmul_mx(
+                    out=acc[:],
+                    lhsT=hq[m][:, g, :].bitcast(FP8X4),
+                    lhsT_scale=hs[m][4 * g : P, :],
+                    rhs=w1q[n][:, g, :].bitcast(FP8X4),
+                    rhs_scale=w1s[n][4 * g : P, :],
+                    start=(g == 0),
+                    stop=(g == NG - 1),
+                )
+            o = work.tile([P, NW], F32, tag="ot", bufs=6)
+            nc.vector.tensor_tensor(out=o[:], in0=acc[:], in1=b1c[n][:], op=ALU.add)
+            nc.scalar.activation(out=o[:], in_=o[:], func=ACT.Gelu)
+            nc.sync.dma_start(out=g_f[P * m : P * (m + 1), cols], in_=o[:])
+
+        nxt = [0] * EARLY
+
+        def early_blocks(m_max, per_chunk):
+            for n in range(EARLY):
+                for rep in range(per_chunk):
+                    if n in ready and nxt[n] <= min(m_max, NT - 1):
+                        block(n, nxt[n])
+                        nxt[n] = nxt[n] + 1
+
         NWO = ND * NG
         for i in range(NT):
             load_tok(i + 2)
@@ -271,54 +309,37 @@ def tile_tinyblock_pb_l_kernel(tc, attn, x, wo, bo, mlp_norm_w, w1, b1, out_0, o
             make_h(i - 1)
             quant_h(i - 2)
             stage1(i, prep_next_wo if i == 0 else nothing)
-            if i >= 3 and i % 2 == 1 and (i - 3) // 2 < 2 * NG:
-                k = NWO + (i - 3) // 2
-                group_unit(k, False)
-                load_unit(k + RAW_BUFS)
-            if i >= 4 and i % 2 == 0 and (i - 4) // 2 < 2 * NG:
-                quant_unit(NWO + (i - 4) // 2)
-            if i == 8:
-                nc.sync.dma_start(out=b1_b[:], in_=b1.partition_broadcast(P))
+            for k in range(NWO, NWO + NG * (EARLY + 1)):
+                j = k - NWO
+                at = 1 + j // 2 if j < NG * EARLY else 14 + (j - NG * EARLY)
+                if i == at:
+                    group_unit(k, False)
+                    load_unit(k + RAW_BUFS)
+                if i == at + 1:
+                    quant_unit(k)
+            early_blocks(i - 3, 2)
 
-        ot = None
-        for n in range(NF):
-            cols = slice(NW * n, NW * (n + 1))
-            for m in range(NT):
-                idx = n * NT + m
-                if idx == 0:
-                    tr_h(NT - 2)
-                    make_h(NT - 1)
-                    quant_h(NT - 2)
-                if idx == 6:
-                    tr_h(NT - 1)
-                    quant_h(NT - 1)
-                if 1 <= n < NF - 1:
-                    k = NWO + NG * (n + 1) + m // 6
-                    if m % 6 == 0:
-                        group_unit(k, (m // 6) % 2 == 0)
-                        load_unit(k + RAW_BUFS)
-                    if m % 6 == 3:
-                        quant_unit(k)
-                acc = psum.tile([P, NW], F32, tag=("acc" if idx % 2 == 0 else "tp"))
-                for g in range(NG):
-                    nc.tensor.matmul_mx(
-                        out=acc[:],
-                        lhsT=hq[m][:, g, :].bitcast(FP8X4),
-                        lhsT_scale=hs[m][4 * g : P, :],
-                        rhs=w1q[n][:, g, :].bitcast(FP8X4),
-                        rhs_scale=w1s[n][4 * g : P, :],
-                        start=(g == 0),
-                        stop=(g == NG - 1),
-                    )
-                q = m % 4
-                if q == 0:
-                    ot = work.tile([P, 4, NW], F32, tag="xm", bufs=3)
-                nc.vector.tensor_tensor(out=ot[:, q, :], in0=acc[:], in1=b1_b[:, cols], op=ALU.add)
-                nc.scalar.activation(out=ot[:, q, :], in_=ot[:, q, :], func=ACT.Gelu)
-                last = n == NF - 1 and m >= NT - 4
-                if last:
-                    nc.sync.dma_start(out=g_f[P * m : P * (m + 1), cols], in_=ot[:, q, :])
-                elif q == 3:
-                    nc.sync.dma_start(
-                        out=g_f[P * (m - 3) : P * (m + 1), cols].rearrange("(q p) c -> p q c", p=P), in_=ot[:]
-                    )
+        tr_h(NT - 2)
+        make_h(NT - 1)
+        quant_h(NT - 2)
+        early_blocks(NT - 3, NT)
+        for m in range(0, 4):
+            block(EARLY, m)
+        tr_h(NT - 1)
+        quant_h(NT - 1)
+        early_blocks(NT - 2, NT)
+        for m in range(4, 8):
+            block(EARLY, m)
+        early_blocks(NT - 1, NT)
+
+        for n in range(EARLY, NF):
+            first = 8 if n == EARLY else 0
+            step = 3 if n == EARLY else 6
+            for m in range(first, NT):
+                if n + 1 < NF and (m - first) % step == 0 and (m - first) // step < NG:
+                    k = NWO + NG * (n + 1) + (m - first) // step
+                    group_unit(k, ((m - first) // step) % 2 == 0)
+                    load_unit(k + RAW_BUFS)
+                if n + 1 < NF and (m - first) % step == 2 and (m - first) // step < NG:
+                    quant_unit(NWO + NG * (n + 1) + (m - first) // step)
+                block(n, m)

@@ -28,6 +28,9 @@ FLOPS = 2 * TOKENS * D * (D + F)
 MANUAL = False
 XB_ON_GPSIMD = False
 RAW_BUFS = 5
+DELAY = 1
+S_EVERY = 2
+V_SHARE = 4
 EARLY = 2
 
 
@@ -269,6 +272,15 @@ def tile_tinyblock_pb_l_kernel(tc, attn, x, wo, bo, mlp_norm_w, w1, b1, out_0, o
         make_xb(0)
 
         count = [0]
+        pend = []
+        late = [False]
+        done = [0]
+
+        def finish_block():
+            o, m, cols = pend[done[0]]
+            done[0] = done[0] + 1
+            nc.scalar.activation(out=o[:], in_=o[:], func=ACT.Gelu)
+            nc.sync.dma_start(out=g_f[P * m : P * (m + 1), cols], in_=o[:])
 
         def block(n, m):
             idx = count[0]
@@ -286,9 +298,14 @@ def tile_tinyblock_pb_l_kernel(tc, attn, x, wo, bo, mlp_norm_w, w1, b1, out_0, o
                     stop=(g == NG - 1),
                 )
             o = work.tile([P, NW], F32, tag="ot", bufs=6)
-            nc.vector.tensor_tensor(out=o[:], in0=acc[:], in1=b1c[n][:], op=ALU.add)
-            nc.scalar.activation(out=o[:], in_=o[:], func=ACT.Gelu)
-            nc.sync.dma_start(out=g_f[P * m : P * (m + 1), cols], in_=o[:])
+            if late[0] and idx % S_EVERY == S_EVERY - 1:
+                nc.scalar.copy(out=o[:], in_=acc[:])
+                nc.vector.tensor_tensor(out=o[:], in0=o[:], in1=b1c[n][:], op=ALU.add)
+            else:
+                nc.vector.tensor_tensor(out=o[:], in0=acc[:], in1=b1c[n][:], op=ALU.add)
+            pend.append((o, m, cols))
+            if len(pend) - done[0] > DELAY:
+                finish_block()
 
         nxt = [0] * EARLY
 
@@ -332,14 +349,17 @@ def tile_tinyblock_pb_l_kernel(tc, attn, x, wo, bo, mlp_norm_w, w1, b1, out_0, o
             block(EARLY, m)
         early_blocks(NT - 1, NT)
 
+        late[0] = True
         for n in range(EARLY, NF):
             first = 8 if n == EARLY else 0
             step = 3 if n == EARLY else 6
             for m in range(first, NT):
                 if n + 1 < NF and (m - first) % step == 0 and (m - first) // step < NG:
                     k = NWO + NG * (n + 1) + (m - first) // step
-                    group_unit(k, ((m - first) // step) % 2 == 0)
+                    group_unit(k, ((m - first) // step) % 4 < V_SHARE)
                     load_unit(k + RAW_BUFS)
                 if n + 1 < NF and (m - first) % step == 2 and (m - first) // step < NG:
                     quant_unit(NWO + NG * (n + 1) + (m - first) // step)
                 block(n, m)
+        while done[0] < len(pend):
+            finish_block()

@@ -28,9 +28,10 @@ FLOPS = 2 * TOKENS * D * (D + F)
 MANUAL = False
 XB_ON_GPSIMD = False
 RAW_BUFS = 5
-DELAY = 1
-S_EVERY = 2
-V_SHARE = 4
+LATE_TAGS = (
+    ("ot", 6), ("xm", 3), ("ot", 6), ("araw", 2), ("ot", 6), ("xraw", 2), ("ot", 6), ("hb", 2),
+    ("xm", 3), ("ot", 6), ("araw", 2), ("ot", 6), ("xraw", 2), ("xm", 3), ("hb", 2),
+)
 EARLY = 2
 
 
@@ -272,15 +273,7 @@ def tile_tinyblock_pb_l_kernel(tc, attn, x, wo, bo, mlp_norm_w, w1, b1, out_0, o
         make_xb(0)
 
         count = [0]
-        pend = []
         late = [False]
-        done = [0]
-
-        def finish_block():
-            o, m, cols = pend[done[0]]
-            done[0] = done[0] + 1
-            nc.scalar.activation(out=o[:], in_=o[:], func=ACT.Gelu)
-            nc.sync.dma_start(out=g_f[P * m : P * (m + 1), cols], in_=o[:])
 
         def block(n, m):
             idx = count[0]
@@ -297,15 +290,11 @@ def tile_tinyblock_pb_l_kernel(tc, attn, x, wo, bo, mlp_norm_w, w1, b1, out_0, o
                     start=(g == 0),
                     stop=(g == NG - 1),
                 )
-            o = work.tile([P, NW], F32, tag="ot", bufs=6)
-            if late[0] and idx % S_EVERY == S_EVERY - 1:
-                nc.scalar.copy(out=o[:], in_=acc[:])
-                nc.vector.tensor_tensor(out=o[:], in0=o[:], in1=b1c[n][:], op=ALU.add)
-            else:
-                nc.vector.tensor_tensor(out=o[:], in0=acc[:], in1=b1c[n][:], op=ALU.add)
-            pend.append((o, m, cols))
-            if len(pend) - done[0] > DELAY:
-                finish_block()
+            tag, bufs = LATE_TAGS[idx % len(LATE_TAGS)] if late[0] else ("ot", 6)
+            o = work.tile([P, NW], F32, tag=tag, bufs=bufs)
+            nc.vector.tensor_tensor(out=o[:], in0=acc[:], in1=b1c[n][:], op=ALU.add)
+            nc.scalar.activation(out=o[:], in_=o[:], func=ACT.Gelu)
+            nc.sync.dma_start(out=g_f[P * m : P * (m + 1), cols], in_=o[:])
 
         nxt = [0] * EARLY
 
@@ -356,10 +345,8 @@ def tile_tinyblock_pb_l_kernel(tc, attn, x, wo, bo, mlp_norm_w, w1, b1, out_0, o
             for m in range(first, NT):
                 if n + 1 < NF and (m - first) % step == 0 and (m - first) // step < NG:
                     k = NWO + NG * (n + 1) + (m - first) // step
-                    group_unit(k, ((m - first) // step) % 4 < V_SHARE)
+                    group_unit(k, ((m - first) // step) % 2 == 0)
                     load_unit(k + RAW_BUFS)
                 if n + 1 < NF and (m - first) % step == 2 and (m - first) // step < NG:
                     quant_unit(NWO + NG * (n + 1) + (m - first) // step)
                 block(n, m)
-        while done[0] < len(pend):
-            finish_block()

import math
from contextlib import ExitStack

import concourse.mybir as mybir
from concourse.masks import make_identity

F32 = mybir.dt.float32
BF16 = mybir.dt.bfloat16
U32 = mybir.dt.uint32
U8 = mybir.dt.uint8
FP8X4 = mybir.dt.float8_e4m3fn_x4
ALU = mybir.AluOpType
ACT = mybir.ActivationFunctionType

P = 128
TOKENS = 3072
D = 2048
F = 8192
EPS = 1e-6
NT = TOKENS // P
NG = D // 512
NW = 512
ND = D // NW
NF = F // NW

FLOPS = 2 * TOKENS * D * (D + F)

MANUAL = False
XB_ON_GPSIMD = False
RAW_BUFS = 5
LATE_TAGS = (
    ("ot", 6), ("xm", 3), ("ot", 6), ("araw", 2), ("ot", 6), ("xraw", 2), ("ot", 6), ("hb", 2),
    ("xm", 3), ("ot", 6), ("araw", 2), ("ot", 6), ("xraw", 2), ("xm", 3), ("hb", 2),
)
EARLY = 2


def tile_tinyblock_pb_l_kernel(tc, attn, x, wo, bo, mlp_norm_w, w1, b1, out_0, out_1):
    nc = tc.nc
    attn_f = attn.flatten_outer_dims()
    x_f = x.flatten_outer_dims()
    xmid_f = out_0.flatten_outer_dims()
    g_f = out_1.flatten_outer_dims()

    with ExitStack() as ctx:
        const = ctx.enter_context(tc.tile_pool(name="const", bufs=1))
        keep = ctx.enter_context(tc.tile_pool(name="keep", bufs=1))
        wst = ctx.enter_context(tc.tile_pool(name="wst", bufs=2))
        work = ctx.enter_context(tc.tile_pool(name="work", bufs=2))
        small = ctx.enter_context(tc.tile_pool(name="small", bufs=4))
        psum = ctx.enter_context(tc.psum_pool(name="psum", bufs=4))
        if MANUAL:
            ctx.enter_context(tc.manual_schedule())

        identf = const.tile([P, P], F32, name="identf")
        make_identity(nc, identf[:])
        neghalf = const.tile([P, 1], F32, name="neghalf")
        nc.gpsimd.memset(neghalf[:], -0.5)
        warm = const.tile([P, 1], F32, name="warm")
        nc.gpsimd.memset(warm[:], 0.0)
        warm2 = const.tile([P, 1], F32, name="warm2")
        nc.scalar.activation(out=warm2[:], in_=warm[:], func=ACT.Gelu)
        junk = const.tile([P, D // 2], BF16, name="junk")
        bo_b = const.tile([P, D], BF16, name="bo_b")
        gain_b = const.tile([P, D], BF16, name="gain_b")

        woq = []
        wos = []
        for n in range(ND):
            woq_t = keep.tile([P, NG, NW], U32, name="woq%d" % n, align_bytes=64)
            wos_t = keep.tile([P, NW], U8, name="wos%d" % n, align_bytes=64)
            woq.append(woq_t)
            wos.append(wos_t)
        hq = []
        hs = []
        for m in range(NT):
            hq_t = keep.tile([P, NG, P], U32, name="hq%d" % m, align_bytes=64)
            hs_t = keep.tile([P, P], U8, name="hs%d" % m, align_bytes=64)
            hq.append(hq_t)
            hs.append(hs_t)

        units = [(0, n, g) for n in range(ND) for g in range(NG)] + [(1, n, g) for n in range(NF) for g in range(NG)]
        raws = {}
        grps = {}
        w1q = {}
        w1s = {}
        b1c = {}
        ready = set()

        def load_unit(k):
            if k >= len(units):
                return
            kind, n, g = units[k]
            src = w1 if kind else wo
            raw = wst.tile([P, 4, NW], BF16, tag="wraw", bufs=RAW_BUFS)
            nc.sync.dma_start(
                out=raw[:],
                in_=src[512 * g : 512 * (g + 1), NW * n : NW * (n + 1)].rearrange("(p j) c -> p j c", j=4),
            )
            raws[k] = raw

        def group_unit(k, on_vector):
            grp = wst.tile([P, NW, 4], BF16, tag="wgrp", bufs=3, align_bytes=64)
            src = raws[k][:].rearrange("p j c -> p c j")
            if on_vector:
                nc.vector.tensor_copy(out=grp[:], in_=src)
            else:
                nc.scalar.copy(out=grp[:], in_=src)
            grps[k] = grp

        def quant_unit(k):
            kind, n, g = units[k]
            if kind:
                if g == 0:
                    wq_t = wst.tile([P, NG, NW], U32, tag="wq", bufs=3, align_bytes=64)
                    ws_t = wst.tile([P, NW], U8, tag="wsc", bufs=3, align_bytes=64)
                    b1_t = wst.tile([P, NW], BF16, tag="b1c", bufs=3)
                    nc.sync.dma_start(out=b1_t[:], in_=b1[NW * n : NW * (n + 1)].partition_broadcast(P))
                    w1q[n] = wq_t
                    w1s[n] = ws_t
                    b1c[n] = b1_t
                q, s = w1q[n], w1s[n]
            else:
                q, s = woq[n], wos[n]
            nc.vector.quantize_mx(
                out=q[:, g, :].bitcast(FP8X4),
                scales=s[4 * g : P, :],
                in_=grps[k][:].rearrange("p c j -> p (c j)"),
            )
            if kind and g == NG - 1:
                ready.add(n)

        araw = {}
        xraw = {}
        agrp = {}
        hgrp = {}
        aq = {}
        asc = {}
        xm = {}
        hb = {}
        rstd = {}

        def load_tok(i):
            if i >= NT:
                return
            ar = work.tile([P, D], BF16, tag="araw", bufs=2)
            nc.sync.dma_start(out=ar[:], in_=attn_f[P * i : P * (i + 1), :])
            xr = work.tile([P, D], BF16, tag="xraw", bufs=2)
            nc.sync.dma_start(out=xr[:], in_=x_f[P * i : P * (i + 1), :])
            araw[i] = ar
            xraw[i] = xr

        def transpose_rows(src):
            words = src[:].bitcast(F32)
            grp = work.tile([P, NG, P, 4], BF16, tag="grp", bufs=3, align_bytes=64)
            grp_w = grp[:].rearrange("p g r t -> p (g r t)").bitcast(F32).rearrange("p (g r u) -> p g r u", g=NG, u=2)
            for b in range(2):
                tp = psum.tile([P, 2, 2, P], F32, tag="tp")
                for gg in range(2):
                    g = 2 * b + gg
                    for u in range(2):
                        nc.tensor.transpose(tp[:, gg, u, :], words[:, 256 * g + u : 256 * (g + 1) : 2], identf[:])
                nc.scalar.copy(out=grp_w[:, 2 * b : 2 * b + 2], in_=tp[:].rearrange("p g u r -> p g r u"))
            return grp

        def tr_a(i):
            if 0 <= i < NT:
                agrp[i] = transpose_rows(araw[i])

        def tr_h(i):
            if 0 <= i < NT:
                hgrp[i] = transpose_rows(hb[i])

        def make_xb(i):
            if not 0 <= i < NT:
                return
            xm_t = work.tile([P, D], F32, tag="xm", bufs=3)
            eng = nc.gpsimd if XB_ON_GPSIMD else nc.vector
            eng.tensor_tensor(out=xm_t[:], in0=xraw[i][:], in1=bo_b[:], op=ALU.add)
            xm[i] = xm_t

        def quant_a(i):
            if not 0 <= i < NT:
                return
            aq_t = work.tile([P, NG * P], U32, tag="aq", bufs=2, align_bytes=64)
            as_t = work.tile([P, NG * P], U8, tag="asc", bufs=2, align_bytes=64)
            nc.vector.quantize_mx(
                out=aq_t[:].bitcast(FP8X4), scales=as_t[:], in_=agrp[i][:].rearrange("p g r t -> p (g r t)")
            )
            aq[i] = aq_t
            asc[i] = as_t

        def make_h(i):
            if not 0 <= i < NT:
                return
            hb_t = work.tile([P, D], BF16, tag="hb", bufs=2)
            nc.vector.scalar_tensor_tensor(
                out=hb_t[:], in0=xm[i][:], scalar=rstd[i][:, 0:1], in1=gain_b[:], op0=ALU.mult, op1=ALU.mult
            )
            hb[i] = hb_t

        def quant_h(i):
            if not 0 <= i < NT:
                return
            for g in range(NG):
                nc.vector.quantize_mx(
                    out=hq[i][:, g, :].bitcast(FP8X4),
                    scales=hs[i][4 * g : P, :],
                    in_=hgrp[i][:, g].rearrange("p r t -> p (r t)"),
                )

        def stage1(i, mid):
            sums = []
            for n in range(ND):
                cols = slice(NW * n, NW * (n + 1))
                acc = psum.tile([P, NW], F32, tag="acc")
                for g in range(NG):
                    nc.tensor.matmul_mx(
                        out=acc[:],
                        lhsT=aq[i][:, P * g : P * (g + 1)].bitcast(FP8X4),
                        lhsT_scale=asc[i][:, P * g : P * (g + 1)],
                        rhs=woq[n][:, g, :].bitcast(FP8X4),
                        rhs_scale=wos[n][4 * g : P, :],
                        start=(g == 0),
                        stop=(g == NG - 1),
                    )
                mid(n)
                nc.vector.tensor_tensor(out=xm[i][:, cols], in0=acc[:], in1=xm[i][:, cols], op=ALU.add)
                if n % 2 == 1:
                    ss = small.tile([P, 1], F32, tag="ss%d" % (n // 2))
                    nc.scalar.activation(
                        out=junk[:],
                        in_=xm[i][:, NW * (n - 1) : NW * (n + 1)],
                        func=ACT.Square,
                        scale=1.0 / math.sqrt(D),
                        accum_out=ss[:],
                    )
                    sums.append(ss)
            var = small.tile([P, 1], F32, tag="var")
            nc.gpsimd.tensor_scalar(
                out=var[:], in0=sums[0][:], scalar1=sums[1][:, 0:1], scalar2=EPS, op0=ALU.add, op1=ALU.add
            )
            rs = small.tile([P, 1], F32, tag="rstd")
            nc.gpsimd.tensor_tensor(out=rs[:], in0=var[:], in1=neghalf[:], op=ALU.pow)
            rstd[i] = rs
            nc.sync.dma_start(out=xmid_f[P * i : P * (i + 1), :], in_=xm[i][:])

        def nothing(n):
            return

        def prep_wo(n):
            for g in range(NG):
                k = NG * n + g
                group_unit(k, g % 2 == 0)
                load_unit(k + RAW_BUFS)
                if g > 0:
                    quant_unit(k - 1)
            quant_unit(NG * n + NG - 1)

        def prep_next_wo(n):
            if n + 1 < ND:
                prep_wo(n + 1)

        load_tok(0)
        for k in range(RAW_BUFS):
            load_unit(k)
        nc.sync.dma_start(out=bo_b[:], in_=bo.partition_broadcast(P))
        load_tok(1)
        nc.sync.dma_start(out=gain_b[:], in_=mlp_norm_w.partition_broadcast(P))
        tr_a(0)
        prep_wo(0)
        quant_a(0)
        make_xb(0)

        count = [0]
        late = [False]

        def block(n, m):
            idx = count[0]
            count[0] = idx + 1
            cols = slice(NW * n, NW * (n + 1))
            acc = psum.tile([P, NW], F32, tag=("acc" if idx % 2 == 0 else "tp"))
            for g in range(NG):
                nc.tensor.matmul_mx(
                    out=acc[:],
                    lhsT=hq[m][:, g, :].bitcast(FP8X4),
                    lhsT_scale=hs[m][4 * g : P, :],
                    rhs=w1q[n][:, g, :].bitcast(FP8X4),
                    rhs_scale=w1s[n][4 * g : P, :],
                    start=(g == 0),
                    stop=(g == NG - 1),
                )
            tag, bufs = LATE_TAGS[idx % len(LATE_TAGS)] if late[0] else ("ot", 6)
            o = work.tile([P, NW], F32, tag=tag, bufs=bufs)
            nc.vector.tensor_tensor(out=o[:], in0=acc[:], in1=b1c[n][:], op=ALU.add)
            nc.scalar.activation(out=o[:], in_=o[:], func=ACT.Gelu)
            nc.sync.dma_start(out=g_f[P * m : P * (m + 1), cols], in_=o[:])

        nxt = [0] * EARLY

        def early_blocks(m_max, per_chunk):
            for n in range(EARLY):
                for rep in range(per_chunk):
                    if n in ready and nxt[n] <= min(m_max, NT - 1):
                        block(n, nxt[n])
                        nxt[n] = nxt[n] + 1

        NWO = ND * NG
        for i in range(NT):
            load_tok(i + 2)
            tr_a(i + 1)
            tr_h(i - 2)
            make_xb(i + 1)
            quant_a(i + 1)
            make_h(i - 1)
            quant_h(i - 2)
            stage1(i, prep_next_wo if i == 0 else nothing)
            for k in range(NWO, NWO + NG * (EARLY + 1)):
                j = k - NWO
                at = 1 + j // 2 if j < NG * EARLY else 14 + (j - NG * EARLY)
                if i == at:
                    group_unit(k, False)
                    load_unit(k + RAW_BUFS)
                if i == at + 1:
                    quant_unit(k)
            early_blocks(i - 3, 2)

        tr_h(NT - 2)
        make_h(NT - 1)
        quant_h(NT - 2)
        early_blocks(NT - 3, NT)
        for m in range(0, 4):
            block(EARLY, m)
        tr_h(NT - 1)
        quant_h(NT - 1)
        early_blocks(NT - 2, NT)
        for m in range(4, 8):
            block(EARLY, m)
        early_blocks(NT - 1, NT)

        late[0] = True
        for n in range(EARLY, NF):
            first = 8 if n == EARLY else 0
            step = 3 if n == EARLY else 6
            for m in range(first, NT):
                if n + 1 < NF and (m - first) % step == 0 and (m - first) // step < NG:
                    k = NWO + NG * (n + 1) + (m - first) // step
                    group_unit(k, ((m - first) // step) % 2 == 0)
                    load_unit(k + RAW_BUFS)
                if n + 1 < NF and (m - first) % step == 2 and (m - first) // step < NG:
                    quant_unit(NWO + NG * (n + 1) + (m - first) // step)
                block(n, m)
